import numpy as np
import ml_dtypes


def mxq(x, axis, fmt="e4m3"):
    dtype, down = {"e4m3": (ml_dtypes.float8_e4m3fn, 7), "e5m2": (ml_dtypes.float8_e5m2, 14)}[fmt]
    v = np.moveaxis(np.asarray(x, np.float32).astype(ml_dtypes.bfloat16).astype(np.float64), axis, -1)
    blocks = v.reshape(v.shape[:-1] + (-1, 32))
    amax = np.abs(blocks).max(-1, keepdims=True)
    byte = np.maximum(np.where(amax > 0, np.frexp(amax)[1] - 1 + 127, 0) - down, 1)
    scale = np.exp2(byte - 127.0)
    codes = (blocks / scale).astype(np.float32).astype(dtype).astype(np.float64)
    return np.moveaxis((codes * scale).reshape(v.shape), -1, axis)


WIDE = False


def mx_kscale(k):
    if not WIDE:
        return np.ones(k)
    levels = np.array([10, -10, 5, -5, 0])
    a = np.random.permutation(np.resize(levels, k // 512 * 4)).reshape(k // 512, 4)
    idx = np.arange(k)
    return np.exp2(a[idx // 512, idx % 128 // 32])


BF16 = ml_dtypes.bfloat16


def bf(x):
    return np.asarray(x, np.float32).astype(BF16)


def f64(x):
    return np.asarray(x).astype(np.float64)


B, R, U, HID, G = 256, 16384, 512, 1024, 256


def sigmoid(v):
    return 1.0 / (1.0 + np.exp(-v))


def setup_inputs():
    s = mx_kscale(R)
    return {"y_tilde": bf(np.random.standard_normal((B, R)) * s),
            "z_next": bf(np.random.standard_normal((B, R)) * s),
            "dt": bf(0.3 + 0.2 * np.random.random(1)),
            "glu_w1": bf(np.random.standard_normal((G, R)) * 1.5 / np.sqrt(R) / s),
            "glu_w2": bf(np.random.standard_normal((G, R)) / np.sqrt(R) / s),
            "glu_b1": bf(np.random.standard_normal(G) * 0.3),
            "glu_b2": bf(np.random.standard_normal(G) * 0.3)}


def reference(y_tilde, z_next, dt, glu_w1, glu_w2, glu_b1, glu_b2):
    y_next = f64(y_tilde) + f64(dt) * f64(z_next)
    yq = mxq(y_next, 1, "e4m3")
    gate = sigmoid((yq @ mxq(f64(glu_w1), 1, "e4m3").T) + f64(glu_b1))
    return gate * ((yq @ mxq(f64(glu_w2), 1, "e4m3").T) + f64(glu_b2))

@@ -1,0 +1,208 @@
+from contextlib import ExitStack
+
+import concourse.mybir as mybir
+from concourse.masks import make_identity
+
+BF16 = mybir.dt.bfloat16
+F32 = mybir.dt.float32
+U32 = mybir.dt.uint32
+U8 = mybir.dt.uint8
+FP8X4 = mybir.dt.float8_e4m3fn_x4
+ALU = mybir.AluOpType
+ACT = mybir.ActivationFunctionType
+
+BATCH, MODES, GATES = 256, 16384, 256
+
+P = 128
+PACK = 4
+K_PASS = P * PACK
+PASSES = MODES // K_PASS
+ROW_TILES = 2
+PAIR_HALVES = 2
+
+CHUNK_PASSES = 4
+CHUNK = CHUNK_PASSES * K_PASS
+CHUNKS = PASSES // CHUNK_PASSES
+HALF_PASSES = CHUNK_PASSES // 2
+HALF = HALF_PASSES * K_PASS
+
+N_OUT = 2 * GATES
+
+FLOPS = 2 * BATCH * MODES * N_OUT
+
+
+def tile_instrumentedlocmblock_pb_k_kernel(
+    tc, y_tilde, z_next, dt, glu_w1, glu_w2, glu_b1, glu_b2, out
+):
+    nc = tc.nc
+    with ExitStack() as ctx:
+        consts = ctx.enter_context(tc.tile_pool(name="consts", bufs=1))
+        loads = ctx.enter_context(tc.tile_pool(name="loads", bufs=3))
+        stage = ctx.enter_context(tc.tile_pool(name="stage", bufs=3))
+        finish = ctx.enter_context(tc.tile_pool(name="finish", bufs=2))
+        banks = ctx.enter_context(tc.psum_pool(name="banks", bufs=6))
+        sums = ctx.enter_context(tc.psum_pool(name="sums", bufs=1))
+        ctx.enter_context(tc.manual_schedule())
+
+        def load(src, c, name):
+            rows = loads.tile([P, ROW_TILES, CHUNK], BF16, name=name)
+            nc.sync.dma_start(
+                out=rows[:],
+                in_=src.rearrange("(a p) k -> p a k", p=P)[:, :, c * CHUNK : (c + 1) * CHUNK],
+            )
+            return rows
+
+        y_rows, z_rows, w1_rows, w2_rows = {}, {}, {}, {}
+
+        def load_positions(c):
+            y_rows[c] = load(y_tilde, c, "y_rows")
+            z_rows[c] = load(z_next, c, "z_rows")
+
+        def load_weights(c):
+            w1_rows[c] = load(glu_w1, c, "w1_rows")
+            w2_rows[c] = load(glu_w2, c, "w2_rows")
+
+        load_positions(0)
+        load_positions(1)
+        load_weights(0)
+
+        dt_bf16 = consts.tile([P, 1], BF16, name="dt_bf16")
+        nc.scalar.dma_start(out=dt_bf16[:], in_=dt.partition_broadcast(P))
+        dt_f32 = consts.tile([P, 1], F32, name="dt_f32")
+        nc.vector.tensor_copy(out=dt_f32[:], in_=dt_bf16[:])
+
+        identity = consts.tile([P, P], F32, name="identity")
+        make_identity(nc, identity[:])
+
+        bias_row = consts.tile([P, N_OUT], BF16, name="bias_row")
+        nc.vector.memset(bias_row[:], 0.0)
+        nc.scalar.dma_start(out=bias_row[0:1, 0:GATES], in_=glu_b1.unsqueeze(0))
+        nc.scalar.dma_start(out=bias_row[0:1, GATES:N_OUT], in_=glu_b2.unsqueeze(0))
+        ones = consts.tile([P, P], BF16, name="ones")
+        nc.vector.memset(ones[:], 1.0)
+        bias_bank = banks.tile([P, N_OUT], F32, name="bias_bank", tag="bank")
+        nc.tensor.matmul(out=bias_bank[:], lhsT=ones[:], rhs=bias_row[:], start=True, stop=True)
+        bias = consts.tile([P, N_OUT], F32, name="bias")
+        nc.scalar.copy(out=bias[:], in_=bias_bank[:])
+
+        table_warmer = consts.tile([P, 1], F32, name="table_warmer")
+        nc.scalar.activation(out=table_warmer[:], in_=dt_f32[:], func=ACT.Sigmoid)
+
+        acc = [sums.tile([P, N_OUT], F32, name="acc%d" % a) for a in range(ROW_TILES)]
+
+        y_next, y_grouped, y_codes, y_scales = {}, {}, {}, {}
+        w_grouped, w_codes, w_scales = {}, {}, {}
+
+        def update_positions(c, h):
+            cols = slice(h * HALF, (h + 1) * HALF)
+            y_next[c, h] = stage.tile([P, ROW_TILES, HALF], BF16, name="y_next")
+            nc.vector.scalar_tensor_tensor(
+                out=y_next[c, h][:],
+                in0=z_rows[c][:, :, cols],
+                scalar=dt_f32[:, 0:1],
+                in1=y_rows[c][:, :, cols],
+                op0=ALU.mult,
+                op1=ALU.add,
+            )
+
+        def transpose_pass(rows, first_mode, grouped_words):
+            bank = banks.tile([P, ROW_TILES, PAIR_HALVES, P], F32, name="bank", tag="bank")
+            first_word = first_mode // 2
+            for a in range(ROW_TILES):
+                words = rows[:, a, :].bitcast(F32)
+                for u in range(PAIR_HALVES):
+                    nc.tensor.transpose(
+                        bank[:, a, u, :],
+                        words[:, first_word + u * P : first_word + (u + 1) * P],
+                        identity[:],
+                    )
+            nc.scalar.copy(out=grouped_words, in_=bank[:].rearrange("p a u r -> p a r u"))
+
+        def transpose_positions(c, h):
+            if h == 0:
+                y_grouped[c] = stage.tile(
+                    [P, CHUNK_PASSES * BATCH * PACK], BF16, name="y_grouped", bufs=2, align_bytes=64
+                )
+            words = y_grouped[c][:].bitcast(F32).rearrange(
+                "p (s a r u) -> p s a r u", s=CHUNK_PASSES, a=ROW_TILES, r=P
+            )
+            for s in range(HALF_PASSES):
+                transpose_pass(y_next[c, h], s * K_PASS, words[:, h * HALF_PASSES + s])
+
+        def transpose_weights(rows, which, c):
+            for h in range(2):
+                if which == 0:
+                    w_grouped[c, h] = stage.tile(
+                        [P, HALF_PASSES * N_OUT * PACK], BF16, name="w_grouped", align_bytes=64
+                    )
+                words = w_grouped[c, h][:].bitcast(F32).rearrange(
+                    "p (s w a r u) -> p s w a r u", s=HALF_PASSES, w=2, a=ROW_TILES, r=P
+                )
+                for s in range(HALF_PASSES):
+                    transpose_pass(rows, (h * HALF_PASSES + s) * K_PASS, words[:, s, which])
+
+        def quantise(grouped, columns, name):
+            codes = stage.tile([P, columns], U32, name=name + "_codes", align_bytes=64)
+            scales = stage.tile([P, columns], U8, name=name + "_scales", align_bytes=64)
+            nc.vector.quantize_mx(out=codes[:].bitcast(FP8X4), scales=scales[:], in_=grouped[:])
+            return codes, scales
+
+        def quantise_positions(c):
+            y_codes[c], y_scales[c] = quantise(y_grouped[c], CHUNK_PASSES * BATCH, "y")
+
+        def quantise_weights(c, h):
+            w_codes[c, h], w_scales[c, h] = quantise(w_grouped[c, h], HALF_PASSES * N_OUT, "w")
+
+        def multiply(c):
+            for s in range(CHUNK_PASSES):
+                g = c * CHUNK_PASSES + s
+                h, s_in_half = divmod(s, HALF_PASSES)
+                n_cols = slice(s_in_half * N_OUT, (s_in_half + 1) * N_OUT)
+                for a in range(ROW_TILES):
+                    m_cols = slice((s * ROW_TILES + a) * P, (s * ROW_TILES + a + 1) * P)
+                    nc.tensor.matmul_mx(
+                        out=acc[a][:],
+                        lhsT=y_codes[c][:, m_cols].bitcast(FP8X4),
+                        lhsT_scale=y_scales[c][:, m_cols],
+                        rhs=w_codes[c, h][:, n_cols].bitcast(FP8X4),
+                        rhs_scale=w_scales[c, h][:, n_cols],
+                        start=(g == 0),
+                        stop=(g == PASSES - 1),
+                    )
+
+        for h in range(2):
+            update_positions(0, h)
+            transpose_positions(0, h)
+        for c in range(CHUNKS):
+            more = c + 1 < CHUNKS
+            if c + 2 < CHUNKS:
+                load_positions(c + 2)
+            if more:
+                load_weights(c + 1)
+                update_positions(c + 1, 0)
+            if c > 0:
+                quantise_weights(c - 1, 0)
+                quantise_weights(c - 1, 1)
+            if more:
+                update_positions(c + 1, 1)
+            quantise_positions(c)
+            transpose_weights(w1_rows[c], 0, c)
+            if more:
+                transpose_positions(c + 1, 0)
+            if c > 0:
+                multiply(c - 1)
+            transpose_weights(w2_rows[c], 1, c)
+            if more:
+                transpose_positions(c + 1, 1)
+        quantise_weights(CHUNKS - 1, 0)
+        quantise_weights(CHUNKS - 1, 1)
+        multiply(CHUNKS - 1)
+
+        for a in range(ROW_TILES):
+            biased = finish.tile([P, N_OUT], F32, name="biased")
+            nc.vector.tensor_tensor(out=biased[:], in0=acc[a][:], in1=bias[:], op=ALU.add)
+            gate = finish.tile([P, GATES], F32, name="gate")
+            nc.scalar.activation(out=gate[:], in_=biased[:, 0:GATES], func=ACT.Sigmoid)
+            result = finish.tile([P, GATES], F32, name="result")
+            nc.vector.tensor_mul(out=result[:], in0=gate[:], in1=biased[:, GATES:N_OUT])
+            nc.sync.dma_start(out=out[a * P : (a + 1) * P, :], in_=result[:])

@@ -26,6 +26,8 @@ CHUNKS = PASSES // CHUNK_PASSES
 HALF_PASSES = CHUNK_PASSES // 2
 HALF = HALF_PASSES * K_PASS
 
+BANKS_PER_PASS = 3
+
 N_OUT = 2 * GATES
 
 FLOPS = 2 * BATCH * MODES * N_OUT
@@ -80,10 +82,6 @@ def tile_instrumentedlocmblock_pb_k_kernel(
         nc.scalar.dma_start(out=bias_row[0:1, GATES:N_OUT], in_=glu_b2.unsqueeze(0))
         ones = consts.tile([P, P], BF16, name="ones")
         nc.vector.memset(ones[:], 1.0)
-        bias_bank = banks.tile([P, N_OUT], F32, name="bias_bank", tag="bank")
-        nc.tensor.matmul(out=bias_bank[:], lhsT=ones[:], rhs=bias_row[:], start=True, stop=True)
-        bias = consts.tile([P, N_OUT], F32, name="bias")
-        nc.scalar.copy(out=bias[:], in_=bias_bank[:])
 
         table_warmer = consts.tile([P, 1], F32, name="table_warmer")
         nc.scalar.activation(out=table_warmer[:], in_=dt_f32[:], func=ACT.Sigmoid)
@@ -118,7 +116,7 @@ def tile_instrumentedlocmblock_pb_k_kernel(
                     )
             nc.scalar.copy(out=grouped_words, in_=bank[:].rearrange("p a u r -> p a r u"))
 
-        def transpose_positions(c, h):
+        def position_banks(c, h):
             if h == 0:
                 y_grouped[c] = stage.tile(
                     [P, CHUNK_PASSES * BATCH * PACK], BF16, name="y_grouped", bufs=2, align_bytes=64
@@ -126,10 +124,13 @@ def tile_instrumentedlocmblock_pb_k_kernel(
             words = y_grouped[c][:].bitcast(F32).rearrange(
                 "p (s a r u) -> p s a r u", s=CHUNK_PASSES, a=ROW_TILES, r=P
             )
-            for s in range(HALF_PASSES):
-                transpose_pass(y_next[c, h], s * K_PASS, words[:, h * HALF_PASSES + s])
+            return [
+                (y_next[c, h], s * K_PASS, words[:, h * HALF_PASSES + s])
+                for s in range(HALF_PASSES)
+            ]
 
-        def transpose_weights(rows, which, c):
+        def weight_banks(rows, which, c):
+            todo = []
             for h in range(2):
                 if which == 0:
                     w_grouped[c, h] = stage.tile(
@@ -139,7 +140,8 @@ def tile_instrumentedlocmblock_pb_k_kernel(
                     "p (s w a r u) -> p s w a r u", s=HALF_PASSES, w=2, a=ROW_TILES, r=P
                 )
                 for s in range(HALF_PASSES):
-                    transpose_pass(rows, (h * HALF_PASSES + s) * K_PASS, words[:, s, which])
+                    todo.append((rows, (h * HALF_PASSES + s) * K_PASS, words[:, s, which]))
+            return todo
 
         def quantise(grouped, columns, name):
             codes = stage.tile([P, columns], U32, name=name + "_codes", align_bytes=64)
@@ -153,26 +155,26 @@ def tile_instrumentedlocmblock_pb_k_kernel(
         def quantise_weights(c, h):
             w_codes[c, h], w_scales[c, h] = quantise(w_grouped[c, h], HALF_PASSES * N_OUT, "w")
 
-        def multiply(c):
-            for s in range(CHUNK_PASSES):
-                g = c * CHUNK_PASSES + s
-                h, s_in_half = divmod(s, HALF_PASSES)
-                n_cols = slice(s_in_half * N_OUT, (s_in_half + 1) * N_OUT)
-                for a in range(ROW_TILES):
-                    m_cols = slice((s * ROW_TILES + a) * P, (s * ROW_TILES + a + 1) * P)
-                    nc.tensor.matmul_mx(
-                        out=acc[a][:],
-                        lhsT=y_codes[c][:, m_cols].bitcast(FP8X4),
-                        lhsT_scale=y_scales[c][:, m_cols],
-                        rhs=w_codes[c, h][:, n_cols].bitcast(FP8X4),
-                        rhs_scale=w_scales[c, h][:, n_cols],
-                        start=(g == 0),
-                        stop=(g == PASSES - 1),
-                    )
+        def multiply_pass(c, s):
+            g = c * CHUNK_PASSES + s
+            h, s_in_half = divmod(s, HALF_PASSES)
+            n_cols = slice(s_in_half * N_OUT, (s_in_half + 1) * N_OUT)
+            for a in range(ROW_TILES):
+                m_cols = slice((s * ROW_TILES + a) * P, (s * ROW_TILES + a + 1) * P)
+                nc.tensor.matmul_mx(
+                    out=acc[a][:],
+                    lhsT=y_codes[c][:, m_cols].bitcast(FP8X4),
+                    lhsT_scale=y_scales[c][:, m_cols],
+                    rhs=w_codes[c, h][:, n_cols].bitcast(FP8X4),
+                    rhs_scale=w_scales[c, h][:, n_cols],
+                    start=(g == 0),
+                    stop=(g == PASSES - 1),
+                )
 
         for h in range(2):
             update_positions(0, h)
-            transpose_positions(0, h)
+            for bank_args in position_banks(0, h):
+                transpose_pass(*bank_args)
         for c in range(CHUNKS):
             more = c + 1 < CHUNKS
             if c + 2 < CHUNKS:
@@ -186,23 +188,41 @@ def tile_instrumentedlocmblock_pb_k_kernel(
             if more:
                 update_positions(c + 1, 1)
             quantise_positions(c)
-            transpose_weights(w1_rows[c], 0, c)
+
+            todo = weight_banks(w1_rows[c], 0, c)
             if more:
-                transpose_positions(c + 1, 0)
+                todo.extend(position_banks(c + 1, 0))
+            todo.extend(weight_banks(w2_rows[c], 1, c))
+            if more:
+                todo.extend(position_banks(c + 1, 1))
+            passes_done = 0
+            for i, bank_args in enumerate(todo):
+                transpose_pass(*bank_args)
+                if c > 0 and (i + 1) % BANKS_PER_PASS == 0:
+                    multiply_pass(c - 1, passes_done)
+                    passes_done += 1
             if c > 0:
-                multiply(c - 1)
-            transpose_weights(w2_rows[c], 1, c)
-            if more:
-                transpose_positions(c + 1, 1)
+                for s in range(passes_done, CHUNK_PASSES):
+                    multiply_pass(c - 1, s)
+
+        bias_bank = banks.tile([P, N_OUT], F32, name="bias_bank", tag="bank")
+        nc.tensor.matmul(out=bias_bank[:], lhsT=ones[:], rhs=bias_row[:], start=True, stop=True)
+        bias = consts.tile([P, N_OUT], F32, name="bias")
+        nc.scalar.copy(out=bias[:], in_=bias_bank[:])
+
         quantise_weights(CHUNKS - 1, 0)
         quantise_weights(CHUNKS - 1, 1)
-        multiply(CHUNKS - 1)
+        for s in range(CHUNK_PASSES):
+            multiply_pass(CHUNKS - 1, s)
 
+        biased, gate = [], []
         for a in range(ROW_TILES):
-            biased = finish.tile([P, N_OUT], F32, name="biased")
-            nc.vector.tensor_tensor(out=biased[:], in0=acc[a][:], in1=bias[:], op=ALU.add)
-            gate = finish.tile([P, GATES], F32, name="gate")
-            nc.scalar.activation(out=gate[:], in_=biased[:, 0:GATES], func=ACT.Sigmoid)
+            biased.append(finish.tile([P, N_OUT], F32, name="biased"))
+            nc.vector.tensor_tensor(out=biased[a][:], in0=acc[a][:], in1=bias[:], op=ALU.add)
+        for a in range(ROW_TILES):
+            gate.append(finish.tile([P, GATES], F32, name="gate"))
+            nc.scalar.activation(out=gate[a][:], in_=biased[a][:, 0:GATES], func=ACT.Sigmoid)
+        for a in range(ROW_TILES):
             result = finish.tile([P, GATES], F32, name="result")
-            nc.vector.tensor_mul(out=result[:], in0=gate[:], in1=biased[:, GATES:N_OUT])
+            nc.vector.tensor_mul(out=result[:], in0=gate[a][:], in1=biased[a][:, GATES:N_OUT])
             nc.sync.dma_start(out=out[a * P : (a + 1) * P, :], in_=result[:])

@@ -26,7 +26,8 @@ CHUNKS = PASSES // CHUNK_PASSES
 HALF_PASSES = CHUNK_PASSES // 2
 HALF = HALF_PASSES * K_PASS
 
-BANKS_PER_PASS = 3
+BANKS_PER_RUN = 4
+PASSES_PER_RUN = 2
 
 N_OUT = 2 * GATES
 
@@ -198,12 +199,10 @@ def tile_instrumentedlocmblock_pb_k_kernel(
             passes_done = 0
             for i, bank_args in enumerate(todo):
                 transpose_pass(*bank_args)
-                if c > 0 and (i + 1) % BANKS_PER_PASS == 0:
-                    multiply_pass(c - 1, passes_done)
-                    passes_done += 1
-            if c > 0:
-                for s in range(passes_done, CHUNK_PASSES):
-                    multiply_pass(c - 1, s)
+                if c > 0 and (i + 1) % BANKS_PER_RUN == 0 and passes_done < CHUNK_PASSES:
+                    for s in range(passes_done, passes_done + PASSES_PER_RUN):
+                        multiply_pass(c - 1, s)
+                    passes_done += PASSES_PER_RUN
 
         bias_bank = banks.tile([P, N_OUT], F32, name="bias_bank", tag="bank")
         nc.tensor.matmul(out=bias_bank[:], lhsT=ones[:], rhs=bias_row[:], start=True, stop=True)

@@ -26,8 +26,7 @@ CHUNKS = PASSES // CHUNK_PASSES
 HALF_PASSES = CHUNK_PASSES // 2
 HALF = HALF_PASSES * K_PASS
 
-BANKS_PER_RUN = 4
-PASSES_PER_RUN = 2
+BANKS_PER_PASS = 3
 
 N_OUT = 2 * GATES
 
@@ -45,7 +44,6 @@ def tile_instrumentedlocmblock_pb_k_kernel(
         finish = ctx.enter_context(tc.tile_pool(name="finish", bufs=2))
         banks = ctx.enter_context(tc.psum_pool(name="banks", bufs=6))
         sums = ctx.enter_context(tc.psum_pool(name="sums", bufs=1))
-        ctx.enter_context(tc.manual_schedule())
 
         def load(src, c, name):
             rows = loads.tile([P, ROW_TILES, CHUNK], BF16, name=name)
@@ -199,10 +197,12 @@ def tile_instrumentedlocmblock_pb_k_kernel(
             passes_done = 0
             for i, bank_args in enumerate(todo):
                 transpose_pass(*bank_args)
-                if c > 0 and (i + 1) % BANKS_PER_RUN == 0 and passes_done < CHUNK_PASSES:
-                    for s in range(passes_done, passes_done + PASSES_PER_RUN):
-                        multiply_pass(c - 1, s)
-                    passes_done += PASSES_PER_RUN
+                if c > 0 and (i + 1) % BANKS_PER_PASS == 0:
+                    multiply_pass(c - 1, passes_done)
+                    passes_done += 1
+            if c > 0:
+                for s in range(passes_done, CHUNK_PASSES):
+                    multiply_pass(c - 1, s)
 
         bias_bank = banks.tile([P, N_OUT], F32, name="bias_bank", tag="bank")
         nc.tensor.matmul(out=bias_bank[:], lhsT=ones[:], rhs=bias_row[:], start=True, stop=True)

from contextlib import ExitStack

import concourse.mybir as mybir
from concourse.masks import make_identity

BF16 = mybir.dt.bfloat16
F32 = mybir.dt.float32
U32 = mybir.dt.uint32
U8 = mybir.dt.uint8
FP8X4 = mybir.dt.float8_e4m3fn_x4
ALU = mybir.AluOpType
ACT = mybir.ActivationFunctionType

BATCH, MODES, GATES = 256, 16384, 256

P = 128
PACK = 4
K_PASS = P * PACK
PASSES = MODES // K_PASS
ROW_TILES = 2
PAIR_HALVES = 2

CHUNK_PASSES = 4
CHUNK = CHUNK_PASSES * K_PASS
CHUNKS = PASSES // CHUNK_PASSES
HALF_PASSES = CHUNK_PASSES // 2
HALF = HALF_PASSES * K_PASS

BANKS_PER_PASS = 3

N_OUT = 2 * GATES

FLOPS = 2 * BATCH * MODES * N_OUT


def tile_instrumentedlocmblock_pb_k_kernel(
    tc, y_tilde, z_next, dt, glu_w1, glu_w2, glu_b1, glu_b2, out
):
    nc = tc.nc
    with ExitStack() as ctx:
        consts = ctx.enter_context(tc.tile_pool(name="consts", bufs=1))
        loads = ctx.enter_context(tc.tile_pool(name="loads", bufs=3))
        stage = ctx.enter_context(tc.tile_pool(name="stage", bufs=3))
        finish = ctx.enter_context(tc.tile_pool(name="finish", bufs=2))
        banks = ctx.enter_context(tc.psum_pool(name="banks", bufs=6))
        sums = ctx.enter_context(tc.psum_pool(name="sums", bufs=1))

        def load(src, c, name):
            rows = loads.tile([P, ROW_TILES, CHUNK], BF16, name=name)
            nc.sync.dma_start(
                out=rows[:],
                in_=src.rearrange("(a p) k -> p a k", p=P)[:, :, c * CHUNK : (c + 1) * CHUNK],
            )
            return rows

        y_rows, z_rows, w1_rows, w2_rows = {}, {}, {}, {}

        def load_positions(c):
            y_rows[c] = load(y_tilde, c, "y_rows")
            z_rows[c] = load(z_next, c, "z_rows")

        def load_weights(c):
            w1_rows[c] = load(glu_w1, c, "w1_rows")
            w2_rows[c] = load(glu_w2, c, "w2_rows")

        load_positions(0)
        load_positions(1)
        load_weights(0)

        dt_bf16 = consts.tile([P, 1], BF16, name="dt_bf16")
        nc.scalar.dma_start(out=dt_bf16[:], in_=dt.partition_broadcast(P))
        dt_f32 = consts.tile([P, 1], F32, name="dt_f32")
        nc.vector.tensor_copy(out=dt_f32[:], in_=dt_bf16[:])

        identity = consts.tile([P, P], F32, name="identity")
        make_identity(nc, identity[:])

        bias_row = consts.tile([P, N_OUT], BF16, name="bias_row")
        nc.vector.memset(bias_row[:], 0.0)
        nc.scalar.dma_start(out=bias_row[0:1, 0:GATES], in_=glu_b1.unsqueeze(0))
        nc.scalar.dma_start(out=bias_row[0:1, GATES:N_OUT], in_=glu_b2.unsqueeze(0))
        ones = consts.tile([P, P], BF16, name="ones")
        nc.vector.memset(ones[:], 1.0)

        table_warmer = consts.tile([P, 1], F32, name="table_warmer")
        nc.scalar.activation(out=table_warmer[:], in_=dt_f32[:], func=ACT.Sigmoid)

        acc = [sums.tile([P, N_OUT], F32, name="acc%d" % a) for a in range(ROW_TILES)]

        y_next, y_grouped, y_codes, y_scales = {}, {}, {}, {}
        w_grouped, w_codes, w_scales = {}, {}, {}

        def update_positions(c, h):
            cols = slice(h * HALF, (h + 1) * HALF)
            y_next[c, h] = stage.tile([P, ROW_TILES, HALF], BF16, name="y_next")
            nc.vector.scalar_tensor_tensor(
                out=y_next[c, h][:],
                in0=z_rows[c][:, :, cols],
                scalar=dt_f32[:, 0:1],
                in1=y_rows[c][:, :, cols],
                op0=ALU.mult,
                op1=ALU.add,
            )

        def transpose_pass(rows, first_mode, grouped_words):
            bank = banks.tile([P, ROW_TILES, PAIR_HALVES, P], F32, name="bank", tag="bank")
            first_word = first_mode // 2
            for a in range(ROW_TILES):
                words = rows[:, a, :].bitcast(F32)
                for u in range(PAIR_HALVES):
                    nc.tensor.transpose(
                        bank[:, a, u, :],
                        words[:, first_word + u * P : first_word + (u + 1) * P],
                        identity[:],
                    )
            nc.scalar.copy(out=grouped_words, in_=bank[:].rearrange("p a u r -> p a r u"))

        def position_banks(c, h):
            if h == 0:
                y_grouped[c] = stage.tile(
                    [P, CHUNK_PASSES * BATCH * PACK], BF16, name="y_grouped", bufs=2, align_bytes=64
                )
            words = y_grouped[c][:].bitcast(F32).rearrange(
                "p (s a r u) -> p s a r u", s=CHUNK_PASSES, a=ROW_TILES, r=P
            )
            return [
                (y_next[c, h], s * K_PASS, words[:, h * HALF_PASSES + s])
                for s in range(HALF_PASSES)
            ]

        def weight_banks(rows, which, c):
            todo = []
            for h in range(2):
                if which == 0:
                    w_grouped[c, h] = stage.tile(
                        [P, HALF_PASSES * N_OUT * PACK], BF16, name="w_grouped", align_bytes=64
                    )
                words = w_grouped[c, h][:].bitcast(F32).rearrange(
                    "p (s w a r u) -> p s w a r u", s=HALF_PASSES, w=2, a=ROW_TILES, r=P
                )
                for s in range(HALF_PASSES):
                    todo.append((rows, (h * HALF_PASSES + s) * K_PASS, words[:, s, which]))
            return todo

        def quantise(grouped, columns, name):
            codes = stage.tile([P, columns], U32, name=name + "_codes", align_bytes=64)
            scales = stage.tile([P, columns], U8, name=name + "_scales", align_bytes=64)
            nc.vector.quantize_mx(out=codes[:].bitcast(FP8X4), scales=scales[:], in_=grouped[:])
            return codes, scales

        def quantise_positions(c):
            y_codes[c], y_scales[c] = quantise(y_grouped[c], CHUNK_PASSES * BATCH, "y")

        def quantise_weights(c, h):
            w_codes[c, h], w_scales[c, h] = quantise(w_grouped[c, h], HALF_PASSES * N_OUT, "w")

        def multiply_pass(c, s):
            g = c * CHUNK_PASSES + s
            h, s_in_half = divmod(s, HALF_PASSES)
            n_cols = slice(s_in_half * N_OUT, (s_in_half + 1) * N_OUT)
            for a in range(ROW_TILES):
                m_cols = slice((s * ROW_TILES + a) * P, (s * ROW_TILES + a + 1) * P)
                nc.tensor.matmul_mx(
                    out=acc[a][:],
                    lhsT=y_codes[c][:, m_cols].bitcast(FP8X4),
                    lhsT_scale=y_scales[c][:, m_cols],
                    rhs=w_codes[c, h][:, n_cols].bitcast(FP8X4),
                    rhs_scale=w_scales[c, h][:, n_cols],
                    start=(g == 0),
                    stop=(g == PASSES - 1),
                )

        for h in range(2):
            update_positions(0, h)
            for bank_args in position_banks(0, h):
                transpose_pass(*bank_args)
        for c in range(CHUNKS):
            more = c + 1 < CHUNKS
            if c + 2 < CHUNKS:
                load_positions(c + 2)
            if more:
                load_weights(c + 1)
                update_positions(c + 1, 0)
            if c > 0:
                quantise_weights(c - 1, 0)
                quantise_weights(c - 1, 1)
            if more:
                update_positions(c + 1, 1)
            quantise_positions(c)

            todo = weight_banks(w1_rows[c], 0, c)
            if more:
                todo.extend(position_banks(c + 1, 0))
            todo.extend(weight_banks(w2_rows[c], 1, c))
            if more:
                todo.extend(position_banks(c + 1, 1))
            passes_done = 0
            for i, bank_args in enumerate(todo):
                transpose_pass(*bank_args)
                if c > 0 and (i + 1) % BANKS_PER_PASS == 0:
                    multiply_pass(c - 1, passes_done)
                    passes_done += 1
            if c > 0:
                for s in range(passes_done, CHUNK_PASSES):
                    multiply_pass(c - 1, s)

        bias_bank = banks.tile([P, N_OUT], F32, name="bias_bank", tag="bank")
        nc.tensor.matmul(out=bias_bank[:], lhsT=ones[:], rhs=bias_row[:], start=True, stop=True)
        bias = consts.tile([P, N_OUT], F32, name="bias")
        nc.scalar.copy(out=bias[:], in_=bias_bank[:])

        quantise_weights(CHUNKS - 1, 0)
        quantise_weights(CHUNKS - 1, 1)
        for s in range(CHUNK_PASSES):
            multiply_pass(CHUNKS - 1, s)

        biased, gate = [], []
        for a in range(ROW_TILES):
            biased.append(finish.tile([P, N_OUT], F32, name="biased"))
            nc.vector.tensor_tensor(out=biased[a][:], in0=acc[a][:], in1=bias[:], op=ALU.add)
        for a in range(ROW_TILES):
            gate.append(finish.tile([P, GATES], F32, name="gate"))
            nc.scalar.activation(out=gate[a][:], in_=biased[a][:, 0:GATES], func=ACT.Sigmoid)
        for a in range(ROW_TILES):
            result = finish.tile([P, GATES], F32, name="result")
            nc.vector.tensor_mul(out=result[:], in0=gate[a][:], in1=biased[a][:, GATES:N_OUT])
            nc.sync.dma_start(out=out[a * P : (a + 1) * P, :], in_=result[:])
